import numpy as np
import ml_dtypes

BF16 = ml_dtypes.bfloat16


def bf(x):
    return np.asarray(x, np.float32).astype(BF16)


def f32(x):
    return np.asarray(x, np.float32)


def f64(x):
    return np.asarray(x).astype(np.float64)


def striped(idx):
    return np.tile(idx.reshape(-1, 16).T, (8, 1))


V, D, M, N, CF = 1024, 128, 512, 512, 4


def setup_inputs():
    return {"emb": bf(np.random.uniform(-0.3, 0.3, (D, V))), "pos": bf(np.random.uniform(-1.0, 1.0, (D, N))), "w": bf(np.random.uniform(-0.15, 0.15, (D, M))), "b": f32(0.1 * np.random.standard_normal((M, 1))), "offs": striped(np.random.permutation(np.tile(np.arange(V), 2))[:N])}


def reference(emb, pos, w, b, offs):
    idx = offs[:16].T.reshape(-1)
    y = np.sqrt(D) * (f64(w).T @ f64(emb)[:, idx]) + f64(w).T @ f64(pos)
    return y.reshape(M, N // CF, CF).mean(axis=2) + f64(b)

@@ -1,0 +1,80 @@
+import math
+
+import concourse.mybir as mybir
+
+P = 128
+WORDS = 1024
+TOKENS = 512
+HEAD = 512
+CHUNK = 4
+POOLED = TOKENS // CHUNK
+BLOCKS = HEAD // P
+WARMUP = 6
+
+FLOPS = 2 * 2 * P * HEAD * TOKENS
+
+BF16, F32, U16 = mybir.dt.bfloat16, mybir.dt.float32, mybir.dt.uint16
+ADD, MULT = mybir.AluOpType.add, mybir.AluOpType.mult
+IDENTITY = mybir.ActivationFunctionType.Identity
+
+
+def tile_poolexpandtransformermodel_kernel(tc, emb, pos, w, b, offs, out):
+    nc = tc.nc
+    with (
+        tc.tile_pool(name="held", bufs=1) as held,
+        tc.tile_pool(name="work", bufs=BLOCKS) as work,
+        tc.psum_pool(name="psum", bufs=BLOCKS) as psum,
+    ):
+        offsets = held.tile([P, TOKENS // 16], U16, name="offsets")
+        table = held.tile([P, WORDS], BF16, name="table")
+        weights = held.tile([P, HEAD], BF16, name="weights")
+        positions = held.tile([P, TOKENS], BF16, name="positions")
+        bias = held.tile([P, BLOCKS], F32, name="bias")
+        zeros = held.tile([P, TOKENS], BF16, name="zeros")
+
+        nc.sync.dma_start(offsets[:], offs)
+        nc.scalar.dma_start(weights[:], w)
+        nc.sync.dma_start(table[:], emb)
+        nc.scalar.dma_start(positions[:], pos)
+        with nc.allow_non_contiguous_dma(reason="512 single float32 values, one to a partition and block"):
+            nc.scalar.dma_start(bias[:], b.rearrange("(g p) o -> p (g o)", p=P))
+
+        nc.vector.memset(zeros[:], 0.0)
+        for i in range(WARMUP):
+            word_product = psum.tile([P, TOKENS], F32, name="word_product")
+            nc.tensor.matmul(word_product[:], zeros[:, 0:P], zeros[:], start=True, stop=True)
+
+        word_products = []
+        for g in range(BLOCKS):
+            word_product = psum.tile([P, TOKENS], F32, name="word_product")
+            nc.tensor.matmul(
+                word_product[:], weights[:, g * P : (g + 1) * P], table[:].indirect(offsets[:]),
+                start=True, stop=True,
+            )
+            word_products.append(word_product)
+
+        word_parts = []
+        for g in range(BLOCKS):
+            word_sum = work.tile([P, POOLED], F32, name="word_sum")
+            nc.vector.tensor_reduce(
+                word_sum[:], word_products[g][:].rearrange("m (t c) -> m t c", c=CHUNK), mybir.AxisListType.X, ADD
+            )
+            word_part = work.tile([P, POOLED], F32, name="word_part")
+            nc.scalar.activation(
+                word_part[:], word_sum[:], IDENTITY, bias=bias[:, g : g + 1], scale=math.sqrt(P) / CHUNK
+            )
+            word_parts.append(word_part)
+
+        positions_by_phase = positions[:].rearrange("k (t c) -> k c t", c=CHUNK)
+        for g in range(BLOCKS):
+            position_sum = psum.tile([P, POOLED], F32, name="position_sum")
+            for c in range(CHUNK):
+                nc.tensor.matmul(
+                    position_sum[:], weights[:, g * P : (g + 1) * P], positions_by_phase[:, c, :],
+                    start=(c == 0), stop=(c == CHUNK - 1),
+                )
+            pooled = work.tile([P, POOLED], F32, name="pooled")
+            nc.vector.scalar_tensor_tensor(
+                pooled[:], position_sum[:], 1.0 / CHUNK, word_parts[g][:], MULT, ADD
+            )
+            nc.sync.dma_start(out[g * P : (g + 1) * P, :], pooled[:])

@@ -9,7 +9,7 @@ HEAD = 512
 CHUNK = 4
 POOLED = TOKENS // CHUNK
 BLOCKS = HEAD // P
-WARMUP = 6
+WARMUP = 4
 
 FLOPS = 2 * 2 * P * HEAD * TOKENS
 

@@ -15,7 +15,6 @@ FLOPS = 2 * 2 * P * HEAD * TOKENS
 
 BF16, F32, U16 = mybir.dt.bfloat16, mybir.dt.float32, mybir.dt.uint16
 ADD, MULT = mybir.AluOpType.add, mybir.AluOpType.mult
-IDENTITY = mybir.ActivationFunctionType.Identity
 
 
 def tile_poolexpandtransformermodel_kernel(tc, emb, pos, w, b, offs, out):
@@ -53,17 +52,13 @@ def tile_poolexpandtransformermodel_kernel(tc, emb, pos, w, b, offs, out):
             )
             word_products.append(word_product)
 
-        word_parts = []
+        word_sums = []
         for g in range(BLOCKS):
             word_sum = work.tile([P, POOLED], F32, name="word_sum")
             nc.vector.tensor_reduce(
                 word_sum[:], word_products[g][:].rearrange("m (t c) -> m t c", c=CHUNK), mybir.AxisListType.X, ADD
             )
-            word_part = work.tile([P, POOLED], F32, name="word_part")
-            nc.scalar.activation(
-                word_part[:], word_sum[:], IDENTITY, bias=bias[:, g : g + 1], scale=math.sqrt(P) / CHUNK
-            )
-            word_parts.append(word_part)
+            word_sums.append(word_sum)
 
         positions_by_phase = positions[:].rearrange("k (t c) -> k c t", c=CHUNK)
         for g in range(BLOCKS):
@@ -73,8 +68,10 @@ def tile_poolexpandtransformermodel_kernel(tc, emb, pos, w, b, offs, out):
                     position_sum[:], weights[:, g * P : (g + 1) * P], positions_by_phase[:, c, :],
                     start=(c == 0), stop=(c == CHUNK - 1),
                 )
-            pooled = work.tile([P, POOLED], F32, name="pooled")
+            chunk_sum = work.tile([P, POOLED], F32, name="chunk_sum")
             nc.vector.scalar_tensor_tensor(
-                pooled[:], position_sum[:], 1.0 / CHUNK, word_parts[g][:], MULT, ADD
+                chunk_sum[:], word_sums[g][:], math.sqrt(P), position_sum[:], MULT, ADD
             )
+            pooled = work.tile([P, POOLED], F32, name="pooled")
+            nc.vector.tensor_scalar(pooled[:], chunk_sum[:], 1.0 / CHUNK, bias[:, g : g + 1], MULT, ADD)
             nc.sync.dma_start(out[g * P : (g + 1) * P, :], pooled[:])

@@ -15,6 +15,7 @@ FLOPS = 2 * 2 * P * HEAD * TOKENS
 
 BF16, F32, U16 = mybir.dt.bfloat16, mybir.dt.float32, mybir.dt.uint16
 ADD, MULT = mybir.AluOpType.add, mybir.AluOpType.mult
+IDENTITY = mybir.ActivationFunctionType.Identity
 
 
 def tile_poolexpandtransformermodel_kernel(tc, emb, pos, w, b, offs, out):
@@ -33,8 +34,9 @@ def tile_poolexpandtransformermodel_kernel(tc, emb, pos, w, b, offs, out):
 
         nc.sync.dma_start(offsets[:], offs)
         nc.scalar.dma_start(weights[:], w)
-        nc.sync.dma_start(table[:], emb)
-        nc.scalar.dma_start(positions[:], pos)
+        nc.sync.dma_start(table[:, 0 : WORDS // 2], emb[:, 0 : WORDS // 2])
+        nc.scalar.dma_start(table[:, WORDS // 2 : WORDS], emb[:, WORDS // 2 : WORDS])
+        nc.sync.dma_start(positions[:], pos)
         with nc.allow_non_contiguous_dma(reason="512 single float32 values, one to a partition and block"):
             nc.scalar.dma_start(bias[:], b.rearrange("(g p) o -> p (g o)", p=P))
 
@@ -52,13 +54,17 @@ def tile_poolexpandtransformermodel_kernel(tc, emb, pos, w, b, offs, out):
             )
             word_products.append(word_product)
 
-        word_sums = []
+        word_parts = []
         for g in range(BLOCKS):
             word_sum = work.tile([P, POOLED], F32, name="word_sum")
             nc.vector.tensor_reduce(
                 word_sum[:], word_products[g][:].rearrange("m (t c) -> m t c", c=CHUNK), mybir.AxisListType.X, ADD
             )
-            word_sums.append(word_sum)
+            word_part = work.tile([P, POOLED], F32, name="word_part")
+            nc.scalar.activation(
+                word_part[:], word_sum[:], IDENTITY, bias=bias[:, g : g + 1], scale=math.sqrt(P) / CHUNK
+            )
+            word_parts.append(word_part)
 
         positions_by_phase = positions[:].rearrange("k (t c) -> k c t", c=CHUNK)
         for g in range(BLOCKS):
@@ -68,10 +74,8 @@ def tile_poolexpandtransformermodel_kernel(tc, emb, pos, w, b, offs, out):
                     position_sum[:], weights[:, g * P : (g + 1) * P], positions_by_phase[:, c, :],
                     start=(c == 0), stop=(c == CHUNK - 1),
                 )
-            chunk_sum = work.tile([P, POOLED], F32, name="chunk_sum")
-            nc.vector.scalar_tensor_tensor(
-                chunk_sum[:], word_sums[g][:], math.sqrt(P), position_sum[:], MULT, ADD
-            )
             pooled = work.tile([P, POOLED], F32, name="pooled")
-            nc.vector.tensor_scalar(pooled[:], chunk_sum[:], 1.0 / CHUNK, bias[:, g : g + 1], MULT, ADD)
+            nc.vector.scalar_tensor_tensor(
+                pooled[:], position_sum[:], 1.0 / CHUNK, word_parts[g][:], MULT, ADD
+            )
             nc.sync.dma_start(out[g * P : (g + 1) * P, :], pooled[:])

@@ -9,7 +9,9 @@ HEAD = 512
 CHUNK = 4
 POOLED = TOKENS // CHUNK
 BLOCKS = HEAD // P
-WARMUP = 4
+EARLY = 2
+WORD_SCALE = math.sqrt(P) / CHUNK
+WARMUP = 3
 
 FLOPS = 2 * 2 * P * HEAD * TOKENS
 
@@ -33,10 +35,11 @@ def tile_poolexpandtransformermodel_kernel(tc, emb, pos, w, b, offs, out):
         zeros = held.tile([P, TOKENS], BF16, name="zeros")
 
         nc.sync.dma_start(offsets[:], offs)
-        nc.scalar.dma_start(weights[:], w)
-        nc.sync.dma_start(table[:, 0 : WORDS // 2], emb[:, 0 : WORDS // 2])
-        nc.scalar.dma_start(table[:, WORDS // 2 : WORDS], emb[:, WORDS // 2 : WORDS])
+        nc.scalar.dma_start(weights[:, 0 : EARLY * P], w[:, 0 : EARLY * P])
         nc.sync.dma_start(positions[:], pos)
+        nc.scalar.dma_start(table[:, WORDS // 2 : WORDS], emb[:, WORDS // 2 : WORDS])
+        nc.sync.dma_start(table[:, 0 : WORDS // 2], emb[:, 0 : WORDS // 2])
+        nc.sync.dma_start(weights[:, EARLY * P : HEAD], w[:, EARLY * P : HEAD])
         with nc.allow_non_contiguous_dma(reason="512 single float32 values, one to a partition and block"):
             nc.scalar.dma_start(bias[:], b.rearrange("(g p) o -> p (g o)", p=P))
 
@@ -44,6 +47,24 @@ def tile_poolexpandtransformermodel_kernel(tc, emb, pos, w, b, offs, out):
         for i in range(WARMUP):
             word_product = psum.tile([P, TOKENS], F32, name="word_product")
             nc.tensor.matmul(word_product[:], zeros[:, 0:P], zeros[:], start=True, stop=True)
+
+        positions_by_phase = positions[:].rearrange("k (t c) -> k c t", c=CHUNK)
+
+        def position_sum_of(g):
+            position_sum = psum.tile([P, POOLED], F32, name="position_sum")
+            for c in range(CHUNK):
+                nc.tensor.matmul(
+                    position_sum[:], weights[:, g * P : (g + 1) * P], positions_by_phase[:, c, :],
+                    start=(c == 0), stop=(c == CHUNK - 1),
+                )
+            return position_sum
+
+        position_parts = []
+        for g in range(EARLY):
+            position_sum = position_sum_of(g)
+            position_part = work.tile([P, POOLED], F32, name="position_part")
+            nc.scalar.activation(position_part[:], position_sum[:], IDENTITY, scale=1.0 / CHUNK)
+            position_parts.append(position_part)
 
         word_products = []
         for g in range(BLOCKS):
@@ -54,28 +75,28 @@ def tile_poolexpandtransformermodel_kernel(tc, emb, pos, w, b, offs, out):
             )
             word_products.append(word_product)
 
-        word_parts = []
-        for g in range(BLOCKS):
+        def word_sum_of(g):
             word_sum = work.tile([P, POOLED], F32, name="word_sum")
             nc.vector.tensor_reduce(
                 word_sum[:], word_products[g][:].rearrange("m (t c) -> m t c", c=CHUNK), mybir.AxisListType.X, ADD
             )
-            word_part = work.tile([P, POOLED], F32, name="word_part")
-            nc.scalar.activation(
-                word_part[:], word_sum[:], IDENTITY, bias=bias[:, g : g + 1], scale=math.sqrt(P) / CHUNK
-            )
-            word_parts.append(word_part)
+            return word_sum
 
-        positions_by_phase = positions[:].rearrange("k (t c) -> k c t", c=CHUNK)
-        for g in range(BLOCKS):
-            position_sum = psum.tile([P, POOLED], F32, name="position_sum")
-            for c in range(CHUNK):
-                nc.tensor.matmul(
-                    position_sum[:], weights[:, g * P : (g + 1) * P], positions_by_phase[:, c, :],
-                    start=(c == 0), stop=(c == CHUNK - 1),
-                )
+        for g in range(EARLY):
+            word_sum = word_sum_of(g)
+            word_part = work.tile([P, POOLED], F32, name="word_part")
+            nc.scalar.activation(word_part[:], word_sum[:], IDENTITY, bias=bias[:, g : g + 1], scale=WORD_SCALE)
             pooled = work.tile([P, POOLED], F32, name="pooled")
-            nc.vector.scalar_tensor_tensor(
-                pooled[:], position_sum[:], 1.0 / CHUNK, word_parts[g][:], MULT, ADD
+            nc.gpsimd.tensor_tensor(pooled[:], word_part[:], position_parts[g][:], ADD)
+            nc.sync.dma_start(out[g * P : (g + 1) * P, :], pooled[:])
+
+        for g in range(EARLY, BLOCKS):
+            position_sum = position_sum_of(g)
+            position_part = work.tile([P, POOLED], F32, name="position_part")
+            nc.scalar.activation(
+                position_part[:], position_sum[:], IDENTITY, bias=bias[:, g : g + 1], scale=1.0 / CHUNK
             )
+            word_sum = word_sum_of(g)
+            pooled = work.tile([P, POOLED], F32, name="pooled")
+            nc.vector.scalar_tensor_tensor(pooled[:], word_sum[:], WORD_SCALE, position_part[:], MULT, ADD)
             nc.sync.dma_start(out[g * P : (g + 1) * P, :], pooled[:])

@@ -34,14 +34,13 @@ def tile_poolexpandtransformermodel_kernel(tc, emb, pos, w, b, offs, out):
         bias = held.tile([P, BLOCKS], F32, name="bias")
         zeros = held.tile([P, TOKENS], BF16, name="zeros")
 
-        nc.sync.dma_start(offsets[:], offs)
-        nc.scalar.dma_start(weights[:, 0 : EARLY * P], w[:, 0 : EARLY * P])
+        nc.sync.dma_start(weights[:, 0 : EARLY * P], w[:, 0 : EARLY * P])
         nc.sync.dma_start(positions[:], pos)
-        nc.scalar.dma_start(table[:, WORDS // 2 : WORDS], emb[:, WORDS // 2 : WORDS])
-        nc.sync.dma_start(table[:, 0 : WORDS // 2], emb[:, 0 : WORDS // 2])
-        nc.sync.dma_start(weights[:, EARLY * P : HEAD], w[:, EARLY * P : HEAD])
+        nc.sync.dma_start(offsets[:], offs)
+        nc.sync.dma_start(table[:], emb)
         with nc.allow_non_contiguous_dma(reason="512 single float32 values, one to a partition and block"):
-            nc.scalar.dma_start(bias[:], b.rearrange("(g p) o -> p (g o)", p=P))
+            nc.sync.dma_start(bias[:], b.rearrange("(g p) o -> p (g o)", p=P))
+        nc.sync.dma_start(weights[:, EARLY * P : HEAD], w[:, EARLY * P : HEAD])
 
         nc.vector.memset(zeros[:], 0.0)
         for i in range(WARMUP):

@@ -11,7 +11,6 @@ POOLED = TOKENS // CHUNK
 BLOCKS = HEAD // P
 EARLY = 2
 WORD_SCALE = math.sqrt(P) / CHUNK
-WARMUP = 3
 
 FLOPS = 2 * 2 * P * HEAD * TOKENS
 
@@ -32,7 +31,6 @@ def tile_poolexpandtransformermodel_kernel(tc, emb, pos, w, b, offs, out):
         weights = held.tile([P, HEAD], BF16, name="weights")
         positions = held.tile([P, TOKENS], BF16, name="positions")
         bias = held.tile([P, BLOCKS], F32, name="bias")
-        zeros = held.tile([P, TOKENS], BF16, name="zeros")
 
         nc.sync.dma_start(weights[:, 0 : EARLY * P], w[:, 0 : EARLY * P])
         nc.sync.dma_start(positions[:], pos)
@@ -41,11 +39,6 @@ def tile_poolexpandtransformermodel_kernel(tc, emb, pos, w, b, offs, out):
         with nc.allow_non_contiguous_dma(reason="512 single float32 values, one to a partition and block"):
             nc.sync.dma_start(bias[:], b.rearrange("(g p) o -> p (g o)", p=P))
         nc.sync.dma_start(weights[:, EARLY * P : HEAD], w[:, EARLY * P : HEAD])
-
-        nc.vector.memset(zeros[:], 0.0)
-        for i in range(WARMUP):
-            word_product = psum.tile([P, TOKENS], F32, name="word_product")
-            nc.tensor.matmul(word_product[:], zeros[:, 0:P], zeros[:], start=True, stop=True)
 
         positions_by_phase = positions[:].rearrange("k (t c) -> k c t", c=CHUNK)
 

@@ -82,13 +82,17 @@ def tile_poolexpandtransformermodel_kernel(tc, emb, pos, w, b, offs, out):
             nc.gpsimd.tensor_tensor(pooled[:], word_part[:], position_parts[g][:], ADD)
             nc.sync.dma_start(out[g * P : (g + 1) * P, :], pooled[:])
 
-        for g in range(EARLY, BLOCKS):
-            position_sum = position_sum_of(g)
-            position_part = work.tile([P, POOLED], F32, name="position_part")
-            nc.scalar.activation(
-                position_part[:], position_sum[:], IDENTITY, bias=bias[:, g : g + 1], scale=1.0 / CHUNK
-            )
-            word_sum = word_sum_of(g)
+        def finish_on_vector(g, sooner, sooner_scale, later, later_scale):
+            sooner_part = work.tile([P, POOLED], F32, name="sooner_part")
+            nc.scalar.activation(sooner_part[:], sooner[:], IDENTITY, bias=bias[:, g : g + 1], scale=sooner_scale)
             pooled = work.tile([P, POOLED], F32, name="pooled")
-            nc.vector.scalar_tensor_tensor(pooled[:], word_sum[:], WORD_SCALE, position_part[:], MULT, ADD)
+            nc.vector.scalar_tensor_tensor(pooled[:], later[:], later_scale, sooner_part[:], MULT, ADD)
             nc.sync.dma_start(out[g * P : (g + 1) * P, :], pooled[:])
+
+        last, before_last = BLOCKS - 1, BLOCKS - 2
+        position_sum_last = position_sum_of(last)
+        position_sum_before_last = position_sum_of(before_last)
+        word_sum_before_last = word_sum_of(before_last)
+        word_sum_last = word_sum_of(last)
+        finish_on_vector(last, position_sum_last, 1.0 / CHUNK, word_sum_last, WORD_SCALE)
+        finish_on_vector(before_last, word_sum_before_last, WORD_SCALE, position_sum_before_last, 1.0 / CHUNK)

@@ -82,9 +82,12 @@ def tile_poolexpandtransformermodel_kernel(tc, emb, pos, w, b, offs, out):
             nc.gpsimd.tensor_tensor(pooled[:], word_part[:], position_parts[g][:], ADD)
             nc.sync.dma_start(out[g * P : (g + 1) * P, :], pooled[:])
 
-        def finish_on_vector(g, sooner, sooner_scale, later, later_scale):
+        def sooner_part_of(g, sooner, sooner_scale):
             sooner_part = work.tile([P, POOLED], F32, name="sooner_part")
             nc.scalar.activation(sooner_part[:], sooner[:], IDENTITY, bias=bias[:, g : g + 1], scale=sooner_scale)
+            return sooner_part
+
+        def finish_on_vector(g, later, later_scale, sooner_part):
             pooled = work.tile([P, POOLED], F32, name="pooled")
             nc.vector.scalar_tensor_tensor(pooled[:], later[:], later_scale, sooner_part[:], MULT, ADD)
             nc.sync.dma_start(out[g * P : (g + 1) * P, :], pooled[:])
@@ -94,5 +97,7 @@ def tile_poolexpandtransformermodel_kernel(tc, emb, pos, w, b, offs, out):
         position_sum_before_last = position_sum_of(before_last)
         word_sum_before_last = word_sum_of(before_last)
         word_sum_last = word_sum_of(last)
-        finish_on_vector(last, position_sum_last, 1.0 / CHUNK, word_sum_last, WORD_SCALE)
-        finish_on_vector(before_last, word_sum_before_last, WORD_SCALE, position_sum_before_last, 1.0 / CHUNK)
+        sooner_part_before_last = sooner_part_of(before_last, word_sum_before_last, WORD_SCALE)
+        sooner_part_last = sooner_part_of(last, position_sum_last, 1.0 / CHUNK)
+        finish_on_vector(last, word_sum_last, WORD_SCALE, sooner_part_last)
+        finish_on_vector(before_last, position_sum_before_last, 1.0 / CHUNK, sooner_part_before_last)

@@ -36,9 +36,9 @@ def tile_poolexpandtransformermodel_kernel(tc, emb, pos, w, b, offs, out):
         nc.sync.dma_start(positions[:], pos)
         nc.sync.dma_start(offsets[:], offs)
         nc.sync.dma_start(table[:], emb)
+        nc.sync.dma_start(weights[:, EARLY * P : HEAD], w[:, EARLY * P : HEAD])
         with nc.allow_non_contiguous_dma(reason="512 single float32 values, one to a partition and block"):
             nc.sync.dma_start(bias[:], b.rearrange("(g p) o -> p (g o)", p=P))
-        nc.sync.dma_start(weights[:, EARLY * P : HEAD], w[:, EARLY * P : HEAD])
 
         positions_by_phase = positions[:].rearrange("k (t c) -> k c t", c=CHUNK)
 

@@ -24,7 +24,8 @@ def tile_poolexpandtransformermodel_kernel(tc, emb, pos, w, b, offs, out):
     with (
         tc.tile_pool(name="held", bufs=1) as held,
         tc.tile_pool(name="work", bufs=BLOCKS) as work,
-        tc.psum_pool(name="psum", bufs=BLOCKS) as psum,
+        tc.psum_pool(name="word_psum", bufs=BLOCKS + 1) as word_psum,
+        tc.psum_pool(name="position_psum", bufs=BLOCKS - 1) as position_psum,
     ):
         offsets = held.tile([P, TOKENS // 16], U16, name="offsets")
         table = held.tile([P, WORDS], BF16, name="table")
@@ -43,7 +44,7 @@ def tile_poolexpandtransformermodel_kernel(tc, emb, pos, w, b, offs, out):
         positions_by_phase = positions[:].rearrange("k (t c) -> k c t", c=CHUNK)
 
         def position_sum_of(g):
-            position_sum = psum.tile([P, POOLED], F32, name="position_sum")
+            position_sum = position_psum.tile([P, POOLED], F32, name="position_sum")
             for c in range(CHUNK):
                 nc.tensor.matmul(
                     position_sum[:], weights[:, g * P : (g + 1) * P], positions_by_phase[:, c, :],
@@ -60,18 +61,27 @@ def tile_poolexpandtransformermodel_kernel(tc, emb, pos, w, b, offs, out):
 
         word_products = []
         for g in range(BLOCKS):
-            word_product = psum.tile([P, TOKENS], F32, name="word_product")
-            nc.tensor.matmul(
-                word_product[:], weights[:, g * P : (g + 1) * P], table[:].indirect(offsets[:]),
-                start=True, stop=True,
-            )
-            word_products.append(word_product)
+            pieces = 2 if g == 0 else 1
+            size = TOKENS // pieces
+            products = []
+            for i in range(pieces):
+                word_product = word_psum.tile([P, size], F32, name="word_product")
+                nc.tensor.matmul(
+                    word_product[:], weights[:, g * P : (g + 1) * P],
+                    table[:].indirect(offsets[:, i * size // 16 : (i + 1) * size // 16]),
+                    start=True, stop=True,
+                )
+                products.append(word_product)
+            word_products.append(products)
 
         def word_sum_of(g):
             word_sum = work.tile([P, POOLED], F32, name="word_sum")
-            nc.vector.tensor_reduce(
-                word_sum[:], word_products[g][:].rearrange("m (t c) -> m t c", c=CHUNK), mybir.AxisListType.X, ADD
-            )
+            chunks = POOLED // len(word_products[g])
+            for i, word_product in enumerate(word_products[g]):
+                nc.vector.tensor_reduce(
+                    word_sum[:, i * chunks : (i + 1) * chunks],
+                    word_product[:].rearrange("m (t c) -> m t c", c=CHUNK), mybir.AxisListType.X, ADD,
+                )
             return word_sum
 
         for g in range(EARLY):

@@ -10,6 +10,10 @@ CHUNK = 4
 POOLED = TOKENS // CHUNK
 BLOCKS = HEAD // P
 EARLY = 2
+HALVES = 2
+LIST_COLUMNS = TOKENS // 16 // HALVES
+POSITION_BANKS = 2
+WORD_BANKS = 8 - POSITION_BANKS
 WORD_SCALE = math.sqrt(P) / CHUNK
 
 FLOPS = 2 * 2 * P * HEAD * TOKENS
@@ -24,8 +28,8 @@ def tile_poolexpandtransformermodel_kernel(tc, emb, pos, w, b, offs, out):
     with (
         tc.tile_pool(name="held", bufs=1) as held,
         tc.tile_pool(name="work", bufs=BLOCKS) as work,
-        tc.psum_pool(name="word_psum", bufs=BLOCKS + 1) as word_psum,
-        tc.psum_pool(name="position_psum", bufs=BLOCKS - 1) as position_psum,
+        tc.psum_pool(name="word_psum", bufs=WORD_BANKS) as word_psum,
+        tc.psum_pool(name="position_psum", bufs=POSITION_BANKS) as position_psum,
     ):
         offsets = held.tile([P, TOKENS // 16], U16, name="offsets")
         table = held.tile([P, WORDS], BF16, name="table")
@@ -59,55 +63,40 @@ def tile_poolexpandtransformermodel_kernel(tc, emb, pos, w, b, offs, out):
             nc.scalar.activation(position_part[:], position_sum[:], IDENTITY, scale=1.0 / CHUNK)
             position_parts.append(position_part)
 
-        word_products = []
+        word_products = {}
         for g in range(BLOCKS):
-            pieces = 2 if g == 0 else 1
-            size = TOKENS // pieces
-            products = []
-            for i in range(pieces):
-                word_product = word_psum.tile([P, size], F32, name="word_product")
+            for h in range(HALVES):
+                word_product = word_psum.tile([P, TOKENS // HALVES], F32, name="word_product")
                 nc.tensor.matmul(
                     word_product[:], weights[:, g * P : (g + 1) * P],
-                    table[:].indirect(offsets[:, i * size // 16 : (i + 1) * size // 16]),
+                    table[:].indirect(offsets[:, h * LIST_COLUMNS : (h + 1) * LIST_COLUMNS]),
                     start=True, stop=True,
                 )
-                products.append(word_product)
-            word_products.append(products)
+                word_products[g, h] = word_product
 
-        def word_sum_of(g):
+        def word_part_of(g):
             word_sum = work.tile([P, POOLED], F32, name="word_sum")
-            chunks = POOLED // len(word_products[g])
-            for i, word_product in enumerate(word_products[g]):
+            word_part = work.tile([P, POOLED], F32, name="word_part")
+            for h in range(HALVES):
+                chunks = slice(h * POOLED // HALVES, (h + 1) * POOLED // HALVES)
                 nc.vector.tensor_reduce(
-                    word_sum[:, i * chunks : (i + 1) * chunks],
-                    word_product[:].rearrange("m (t c) -> m t c", c=CHUNK), mybir.AxisListType.X, ADD,
+                    word_sum[:, chunks],
+                    word_products[g, h][:].rearrange("m (t c) -> m t c", c=CHUNK), mybir.AxisListType.X, ADD,
                 )
-            return word_sum
+                nc.scalar.activation(
+                    word_part[:, chunks], word_sum[:, chunks], IDENTITY, bias=bias[:, g : g + 1], scale=WORD_SCALE
+                )
+            return word_part
 
         for g in range(EARLY):
-            word_sum = word_sum_of(g)
-            word_part = work.tile([P, POOLED], F32, name="word_part")
-            nc.scalar.activation(word_part[:], word_sum[:], IDENTITY, bias=bias[:, g : g + 1], scale=WORD_SCALE)
+            word_part = word_part_of(g)
             pooled = work.tile([P, POOLED], F32, name="pooled")
             nc.gpsimd.tensor_tensor(pooled[:], word_part[:], position_parts[g][:], ADD)
             nc.sync.dma_start(out[g * P : (g + 1) * P, :], pooled[:])
 
-        def sooner_part_of(g, sooner, sooner_scale):
-            sooner_part = work.tile([P, POOLED], F32, name="sooner_part")
-            nc.scalar.activation(sooner_part[:], sooner[:], IDENTITY, bias=bias[:, g : g + 1], scale=sooner_scale)
-            return sooner_part
-
-        def finish_on_vector(g, later, later_scale, sooner_part):
+        late_position_sums = [position_sum_of(g) for g in range(EARLY, BLOCKS)]
+        late_word_parts = [word_part_of(g) for g in range(EARLY, BLOCKS)]
+        for g, position_sum, word_part in zip(range(EARLY, BLOCKS), late_position_sums, late_word_parts):
             pooled = work.tile([P, POOLED], F32, name="pooled")
-            nc.vector.scalar_tensor_tensor(pooled[:], later[:], later_scale, sooner_part[:], MULT, ADD)
+            nc.vector.scalar_tensor_tensor(pooled[:], position_sum[:], 1.0 / CHUNK, word_part[:], MULT, ADD)
             nc.sync.dma_start(out[g * P : (g + 1) * P, :], pooled[:])
-
-        last, before_last = BLOCKS - 1, BLOCKS - 2
-        position_sum_last = position_sum_of(last)
-        position_sum_before_last = position_sum_of(before_last)
-        word_sum_before_last = word_sum_of(before_last)
-        word_sum_last = word_sum_of(last)
-        sooner_part_before_last = sooner_part_of(before_last, word_sum_before_last, WORD_SCALE)
-        sooner_part_last = sooner_part_of(last, position_sum_last, 1.0 / CHUNK)
-        finish_on_vector(last, word_sum_last, WORD_SCALE, sooner_part_last)
-        finish_on_vector(before_last, position_sum_before_last, 1.0 / CHUNK, sooner_part_before_last)

import math

import concourse.mybir as mybir

P = 128
WORDS = 1024
TOKENS = 512
HEAD = 512
CHUNK = 4
POOLED = TOKENS // CHUNK
BLOCKS = HEAD // P
EARLY = 2
HALVES = 2
LIST_COLUMNS = TOKENS // 16 // HALVES
POSITION_BANKS = 2
WORD_BANKS = 8 - POSITION_BANKS
WORD_SCALE = math.sqrt(P) / CHUNK

FLOPS = 2 * 2 * P * HEAD * TOKENS

BF16, F32, U16 = mybir.dt.bfloat16, mybir.dt.float32, mybir.dt.uint16
ADD, MULT = mybir.AluOpType.add, mybir.AluOpType.mult
IDENTITY = mybir.ActivationFunctionType.Identity


def tile_poolexpandtransformermodel_kernel(tc, emb, pos, w, b, offs, out):
    nc = tc.nc
    with (
        tc.tile_pool(name="held", bufs=1) as held,
        tc.tile_pool(name="work", bufs=BLOCKS) as work,
        tc.psum_pool(name="word_psum", bufs=WORD_BANKS) as word_psum,
        tc.psum_pool(name="position_psum", bufs=POSITION_BANKS) as position_psum,
    ):
        offsets = held.tile([P, TOKENS // 16], U16, name="offsets")
        table = held.tile([P, WORDS], BF16, name="table")
        weights = held.tile([P, HEAD], BF16, name="weights")
        positions = held.tile([P, TOKENS], BF16, name="positions")
        bias = held.tile([P, BLOCKS], F32, name="bias")

        nc.sync.dma_start(weights[:, 0 : EARLY * P], w[:, 0 : EARLY * P])
        nc.sync.dma_start(positions[:], pos)
        nc.sync.dma_start(offsets[:], offs)
        nc.sync.dma_start(table[:], emb)
        nc.sync.dma_start(weights[:, EARLY * P : HEAD], w[:, EARLY * P : HEAD])
        with nc.allow_non_contiguous_dma(reason="512 single float32 values, one to a partition and block"):
            nc.sync.dma_start(bias[:], b.rearrange("(g p) o -> p (g o)", p=P))

        positions_by_phase = positions[:].rearrange("k (t c) -> k c t", c=CHUNK)

        def position_sum_of(g):
            position_sum = position_psum.tile([P, POOLED], F32, name="position_sum")
            for c in range(CHUNK):
                nc.tensor.matmul(
                    position_sum[:], weights[:, g * P : (g + 1) * P], positions_by_phase[:, c, :],
                    start=(c == 0), stop=(c == CHUNK - 1),
                )
            return position_sum

        position_parts = []
        for g in range(EARLY):
            position_sum = position_sum_of(g)
            position_part = work.tile([P, POOLED], F32, name="position_part")
            nc.scalar.activation(position_part[:], position_sum[:], IDENTITY, scale=1.0 / CHUNK)
            position_parts.append(position_part)

        word_products = {}
        for g in range(BLOCKS):
            for h in range(HALVES):
                word_product = word_psum.tile([P, TOKENS // HALVES], F32, name="word_product")
                nc.tensor.matmul(
                    word_product[:], weights[:, g * P : (g + 1) * P],
                    table[:].indirect(offsets[:, h * LIST_COLUMNS : (h + 1) * LIST_COLUMNS]),
                    start=True, stop=True,
                )
                word_products[g, h] = word_product

        def word_part_of(g):
            word_sum = work.tile([P, POOLED], F32, name="word_sum")
            word_part = work.tile([P, POOLED], F32, name="word_part")
            for h in range(HALVES):
                chunks = slice(h * POOLED // HALVES, (h + 1) * POOLED // HALVES)
                nc.vector.tensor_reduce(
                    word_sum[:, chunks],
                    word_products[g, h][:].rearrange("m (t c) -> m t c", c=CHUNK), mybir.AxisListType.X, ADD,
                )
                nc.scalar.activation(
                    word_part[:, chunks], word_sum[:, chunks], IDENTITY, bias=bias[:, g : g + 1], scale=WORD_SCALE
                )
            return word_part

        for g in range(EARLY):
            word_part = word_part_of(g)
            pooled = work.tile([P, POOLED], F32, name="pooled")
            nc.gpsimd.tensor_tensor(pooled[:], word_part[:], position_parts[g][:], ADD)
            nc.sync.dma_start(out[g * P : (g + 1) * P, :], pooled[:])

        late_position_sums = [position_sum_of(g) for g in range(EARLY, BLOCKS)]
        late_word_parts = [word_part_of(g) for g in range(EARLY, BLOCKS)]
        for g, position_sum, word_part in zip(range(EARLY, BLOCKS), late_position_sums, late_word_parts):
            pooled = work.tile([P, POOLED], F32, name="pooled")
            nc.vector.scalar_tensor_tensor(pooled[:], position_sum[:], 1.0 / CHUNK, word_part[:], MULT, ADD)
            nc.sync.dma_start(out[g * P : (g + 1) * P, :], pooled[:])
